import numpy as np
import ml_dtypes


def mxq(x, axis, fmt="e4m3"):
    dtype, down = {"e4m3": (ml_dtypes.float8_e4m3fn, 7), "e5m2": (ml_dtypes.float8_e5m2, 14)}[fmt]
    v = np.moveaxis(np.asarray(x, np.float32).astype(ml_dtypes.bfloat16).astype(np.float64), axis, -1)
    blocks = v.reshape(v.shape[:-1] + (-1, 32))
    amax = np.abs(blocks).max(-1, keepdims=True)
    byte = np.maximum(np.where(amax > 0, np.frexp(amax)[1] - 1 + 127, 0) - down, 1)
    scale = np.exp2(byte - 127.0)
    codes = (blocks / scale).astype(np.float32).astype(dtype).astype(np.float64)
    return np.moveaxis((codes * scale).reshape(v.shape), -1, axis)


WIDE = False


def mx_kscale(k):
    if not WIDE:
        return np.ones(k)
    levels = np.array([10, -10, 5, -5, 0])
    a = np.random.permutation(np.resize(levels, k // 512 * 4)).reshape(k // 512, 4)
    idx = np.arange(k)
    return np.exp2(a[idx // 512, idx % 128 // 32])


BF16 = ml_dtypes.bfloat16


def bf(x):
    return np.asarray(x, np.float32).astype(BF16)


def f64(x):
    return np.asarray(x).astype(np.float64)


B, T, D, K, CD, CF, M = 8, 16, 1024, 4, 128, 512, 256
LN_EPS = 1e-5


def setup_inputs():
    s = mx_kscale(D)
    t = mx_kscale(CF)
    return {
        "h": bf(np.random.standard_normal((B, T, D)) * s),
        "mu_w1_h": bf(np.random.standard_normal((D, CF)) / np.sqrt(D) / s[:, None]),
        "code_mu": bf(np.random.standard_normal((K, CF)) * 0.4),
        "mu_b1": bf(np.random.standard_normal(CF) * 0.2),
        "ln_g": bf((1.0 + 0.1 * np.random.standard_normal(CF)) * t),
        "ln_b": bf(np.random.standard_normal(CF) * 0.2 * t),
        "mu_w2": bf(np.random.standard_normal((CF, CF)) / np.sqrt(CF) / t[:, None]),
        "mu_b2": bf(np.random.standard_normal(CF) * 0.2),
    }


def reference(h, mu_w1_h, code_mu, mu_b1, ln_g, ln_b, mu_w2, mu_b2):
    hp = mxq(f64(h), 2, "e4m3") @ mxq(f64(mu_w1_h), 0, "e4m3")
    mu_pre = hp[:, :, None, :] + f64(code_mu) + f64(mu_b1)
    mean = mu_pre.mean(-1, keepdims=True)
    var = np.square(mu_pre - mean).mean(-1, keepdims=True)
    mu_ln = (mu_pre - mean) * (1.0 / np.sqrt(var + LN_EPS)) * f64(ln_g) + f64(ln_b)
    return np.tanh((mxq(mu_ln, 3, "e4m3") @ mxq(f64(mu_w2), 0, "e4m3")) + f64(mu_b2))

@@ -1,0 +1,201 @@
+from contextlib import ExitStack
+
+import concourse.mybir as mybir
+from concourse.masks import make_identity
+
+F32 = mybir.dt.float32
+BF16 = mybir.dt.bfloat16
+U32 = mybir.dt.uint32
+U8 = mybir.dt.uint8
+FP8X4 = mybir.dt.float8_e4m3fn_x4
+ALU = mybir.AluOpType
+ACT = mybir.ActivationFunctionType
+
+P = 128
+PACK = 4
+D = 1024
+PASSES1 = D // (P * PACK)
+CODES = 4
+CF = 512
+LN_EPS = 1e-5
+
+FLOPS = 2 * P * D * CF + 2 * P * CODES * CF * CF
+
+
+def regroup(copy, grouped, rows):
+    copy(
+        out=grouped.rearrange("p (c i) j -> p c j i", i=4),
+        in_=rows.rearrange("p j (c i) -> p c j i", i=4),
+    )
+
+
+def tile_mixtureconfounderprior_pa_s_kernel(
+    tc, h, mu_w1_h, code_mu, mu_b1, ln_g, ln_b, mu_w2, mu_b2, out
+):
+    nc = tc.nc
+    h_rows = h.flatten_outer_dims()
+    out_rows = out.rearrange("b t k n -> (b t) k n")
+
+    with ExitStack() as pools:
+        keep = pools.enter_context(tc.tile_pool(name="keep", bufs=1))
+        psum_once = pools.enter_context(tc.psum_pool(name="psum_once", bufs=1))
+        psum_turn = pools.enter_context(tc.psum_pool(name="psum_turn", bufs=2))
+        psum_out = pools.enter_context(tc.psum_pool(name="psum_out", bufs=2))
+
+        h_sb = keep.tile([P, D], BF16)
+        nc.sync.dma_start(out=h_sb[:], in_=h_rows)
+        w1_rows = keep.tile([P, PASSES1, PACK, CF], BF16)
+        w1_view = mu_w1_h.rearrange("(g u q e) n -> g q u (e n)", g=PASSES1, u=2, e=2)
+        for g in range(PASSES1):
+            nc.sync.dma_start(
+                out=w1_rows[:, g].rearrange("p (u e) n -> p u (e n)", u=2), in_=w1_view[g]
+            )
+        w2_rows = keep.tile([P, PACK, CF], BF16)
+        nc.sync.dma_start(out=w2_rows[:], in_=mu_w2.rearrange("(c p) n -> p c n", p=P))
+
+        b1_all = keep.tile([P, CF], BF16)
+        nc.scalar.dma_start(out=b1_all[:], in_=mu_b1.partition_broadcast(P))
+        code_all = keep.tile([P, CODES, CF], BF16)
+        nc.scalar.dma_start(
+            out=code_all[:].rearrange("p k f -> p (k f)"),
+            in_=code_mu.rearrange("k f -> (k f)").partition_broadcast(P),
+        )
+        g_all = keep.tile([P, CF], BF16)
+        nc.scalar.dma_start(out=g_all[:], in_=ln_g.partition_broadcast(P))
+        b_all = keep.tile([P, CF], BF16)
+        nc.scalar.dma_start(out=b_all[:], in_=ln_b.partition_broadcast(P))
+        b2_all = keep.tile([P, CF], BF16)
+        nc.scalar.dma_start(out=b2_all[:], in_=mu_b2.partition_broadcast(P))
+
+        ident_f32 = keep.tile([P, P], F32)
+        make_identity(nc, ident_f32[:])
+        ident_bf16 = keep.tile([P, P], BF16)
+        make_identity(nc, ident_bf16[:])
+        minus_half = keep.tile([P, 1], F32)
+        nc.gpsimd.memset(minus_half[:], -0.5)
+
+        h_words = h_sb[:].bitcast(F32)
+        hT_ps = psum_once.tile([P, PASSES1, 2, P], F32)
+        for g in range(PASSES1):
+            for u in range(2):
+                first = (2 * g + u) * P
+                nc.tensor.transpose(hT_ps[:, g, u, :], h_words[:, first : first + P], ident_f32[:])
+        h_grouped = keep.tile([P, PASSES1 * P * PACK], BF16, align_bytes=64)
+        nc.vector.tensor_copy(
+            out=h_grouped[:].bitcast(F32).rearrange("p (g t u) -> p g t u", g=PASSES1, u=2),
+            in_=hT_ps[:].rearrange("p g u t -> p g t u"),
+        )
+        h_codes = keep.tile([P, PASSES1 * P], U32, align_bytes=64)
+        h_scales = keep.tile([P, PASSES1 * P], U8, align_bytes=64)
+        nc.vector.quantize_mx(out=h_codes[:].bitcast(FP8X4), scales=h_scales[:], in_=h_grouped[:])
+
+        w1_grouped = keep.tile([P, PASSES1, CF, PACK], BF16, align_bytes=64)
+        w1_codes = keep.tile([P, PASSES1, CF], U32, align_bytes=64)
+        w1_scales = keep.tile([P, PASSES1, CF], U8, align_bytes=64)
+        for g in range(PASSES1):
+            regroup(nc.vector.tensor_copy, w1_grouped[:, g], w1_rows[:, g])
+        for g in range(PASSES1):
+            nc.vector.quantize_mx(
+                out=w1_codes[:, g, :].bitcast(FP8X4),
+                scales=w1_scales[:, g, :],
+                in_=w1_grouped[:, g].rearrange("p n j -> p (n j)"),
+            )
+        w2_grouped = keep.tile([P, CF, PACK], BF16, align_bytes=64)
+        w2_codes = keep.tile([P, CF], U32, align_bytes=64)
+        w2_scales = keep.tile([P, CF], U8, align_bytes=64)
+        regroup(nc.scalar.copy, w2_grouped[:], w2_rows[:])
+        nc.vector.quantize_mx(
+            out=w2_codes[:].bitcast(FP8X4),
+            scales=w2_scales[:],
+            in_=w2_grouped[:].rearrange("p n j -> p (n j)"),
+        )
+
+        hp_ps = psum_once.tile([P, CF], F32)
+        for g in range(PASSES1):
+            nc.tensor.matmul_mx(
+                out=hp_ps[:],
+                lhsT=h_codes[:, g * P : (g + 1) * P].bitcast(FP8X4),
+                lhsT_scale=h_scales[:, g * P : (g + 1) * P],
+                rhs=w1_codes[:, g, :].bitcast(FP8X4),
+                rhs_scale=w1_scales[:, g, :],
+                start=(g == 0),
+                stop=(g == PASSES1 - 1),
+            )
+
+        hp_b1 = keep.tile([P, CF], F32)
+        nc.vector.tensor_tensor(out=hp_b1[:], in0=hp_ps[:], in1=b1_all[:], op=ALU.add)
+        mu_pre = keep.tile([P, CODES, CF], F32)
+        row_sum = keep.tile([P, CODES], F32)
+        for k in range(CODES):
+            nc.vector.scalar_tensor_tensor(
+                out=mu_pre[:, k, :],
+                in0=hp_b1[:],
+                scalar=1.0,
+                in1=code_all[:, k, :],
+                op0=ALU.mult,
+                op1=ALU.add,
+                accum_out=row_sum[:, k : k + 1],
+            )
+        neg_mean = keep.tile([P, CODES], F32)
+        squares = keep.tile([P, CODES, CF], BF16)
+        sq_sum = keep.tile([P, CODES], F32)
+        var_eps = keep.tile([P, CODES], F32)
+        rstd = keep.tile([P, CODES], F32)
+        for k in range(CODES):
+            one = slice(k, k + 1)
+            nc.gpsimd.tensor_scalar(
+                out=neg_mean[:, one], in0=row_sum[:, one],
+                scalar1=-1.0 / CF, scalar2=0.0, op0=ALU.mult, op1=ALU.add,
+            )
+            nc.scalar.activation(
+                out=squares[:, k, :], in_=mu_pre[:, k, :], func=ACT.Square,
+                bias=neg_mean[:, one], scale=1.0, accum_out=sq_sum[:, one],
+            )
+            nc.gpsimd.tensor_scalar(
+                out=var_eps[:, one], in0=sq_sum[:, one],
+                scalar1=1.0 / CF, scalar2=LN_EPS, op0=ALU.mult, op1=ALU.add,
+            )
+            nc.gpsimd.tensor_tensor(
+                out=rstd[:, one], in0=var_eps[:, one], in1=minus_half[:], op=ALU.pow
+            )
+
+        centred_g = keep.tile([P, CODES, CF], F32)
+        for k in range(CODES):
+            nc.vector.scalar_tensor_tensor(
+                out=centred_g[:, k, :], in0=mu_pre[:, k, :], scalar=neg_mean[:, k : k + 1],
+                in1=g_all[:], op0=ALU.add, op1=ALU.mult,
+            )
+        mu_ln = keep.tile([P, CODES, CF], BF16)
+        ln_grouped = keep.tile([P, CODES, P, PACK], BF16, align_bytes=64)
+        ln_codes = keep.tile([P, CODES, P], U32, align_bytes=64)
+        ln_scales = keep.tile([P, CODES, P], U8, align_bytes=64)
+        result = keep.tile([P, CODES, CF], F32)
+        for k in range(CODES):
+            nc.vector.scalar_tensor_tensor(
+                out=mu_ln[:, k, :], in0=centred_g[:, k, :], scalar=rstd[:, k : k + 1],
+                in1=b_all[:], op0=ALU.mult, op1=ALU.add,
+            )
+            lnT_ps = psum_turn.tile([P, PACK, P], BF16)
+            for c in range(PACK):
+                nc.tensor.transpose(
+                    lnT_ps[:, c, :], mu_ln[:, k, c * P : (c + 1) * P], ident_bf16[:]
+                )
+            nc.scalar.copy(out=ln_grouped[:, k], in_=lnT_ps[:].rearrange("p c t -> p t c"))
+            nc.vector.quantize_mx(
+                out=ln_codes[:, k, :].bitcast(FP8X4),
+                scales=ln_scales[:, k, :],
+                in_=ln_grouped[:, k].rearrange("p t c -> p (t c)"),
+            )
+            out_ps = psum_out.tile([P, CF], F32)
+            nc.tensor.matmul_mx(
+                out=out_ps[:],
+                lhsT=ln_codes[:, k, :].bitcast(FP8X4),
+                lhsT_scale=ln_scales[:, k, :],
+                rhs=w2_codes[:].bitcast(FP8X4),
+                rhs_scale=w2_scales[:],
+                start=True,
+                stop=True,
+            )
+            nc.vector.tensor_tensor(out=result[:, k, :], in0=out_ps[:], in1=b2_all[:], op=ALU.add)
+            nc.scalar.activation(out=result[:, k, :], in_=result[:, k, :], func=ACT.Tanh)
+            nc.sync.dma_start(out=out_rows[:, k, :], in_=result[:, k, :])

@@ -19,6 +19,10 @@ CODES = 4
 CF = 512
 LN_EPS = 1e-5
 
+ROW_G, ROW_B, ROW_B2, ROW_B1 = 4, 5, 6, 7
+VECTORS = 8
+SPREAD = 7
+
 FLOPS = 2 * P * D * CF + 2 * P * CODES * CF * CF
 
 
@@ -39,8 +43,8 @@ def tile_mixtureconfounderprior_pa_s_kernel(
     with ExitStack() as pools:
         keep = pools.enter_context(tc.tile_pool(name="keep", bufs=1))
         psum_once = pools.enter_context(tc.psum_pool(name="psum_once", bufs=1))
-        psum_turn = pools.enter_context(tc.psum_pool(name="psum_turn", bufs=2))
-        psum_out = pools.enter_context(tc.psum_pool(name="psum_out", bufs=2))
+        psum_turn = pools.enter_context(tc.psum_pool(name="psum_turn", bufs=3))
+        psum_out = pools.enter_context(tc.psum_pool(name="psum_out", bufs=3))
 
         h_sb = keep.tile([P, D], BF16)
         nc.sync.dma_start(out=h_sb[:], in_=h_rows)
@@ -53,26 +57,43 @@ def tile_mixtureconfounderprior_pa_s_kernel(
         w2_rows = keep.tile([P, PACK, CF], BF16)
         nc.sync.dma_start(out=w2_rows[:], in_=mu_w2.rearrange("(c p) n -> p c n", p=P))
 
-        b1_all = keep.tile([P, CF], BF16)
-        nc.scalar.dma_start(out=b1_all[:], in_=mu_b1.partition_broadcast(P))
-        code_all = keep.tile([P, CODES, CF], BF16)
-        nc.scalar.dma_start(
-            out=code_all[:].rearrange("p k f -> p (k f)"),
-            in_=code_mu.rearrange("k f -> (k f)").partition_broadcast(P),
-        )
-        g_all = keep.tile([P, CF], BF16)
-        nc.scalar.dma_start(out=g_all[:], in_=ln_g.partition_broadcast(P))
-        b_all = keep.tile([P, CF], BF16)
-        nc.scalar.dma_start(out=b_all[:], in_=ln_b.partition_broadcast(P))
-        b2_all = keep.tile([P, CF], BF16)
-        nc.scalar.dma_start(out=b2_all[:], in_=mu_b2.partition_broadcast(P))
+        vec_rows = keep.tile([P, CF], BF16)
+        nc.vector.memset(vec_rows[:], 0.0)
+        nc.scalar.dma_start(out=vec_rows[0:CODES, :], in_=code_mu)
+        for row, vector in ((ROW_B1, mu_b1), (ROW_G, ln_g), (ROW_B, ln_b), (ROW_B2, mu_b2)):
+            nc.scalar.dma_start(out=vec_rows[row : row + 1, :], in_=vector.unsqueeze(0))
 
-        ident_f32 = keep.tile([P, P], F32)
-        make_identity(nc, ident_f32[:])
         ident_bf16 = keep.tile([P, P], BF16)
         make_identity(nc, ident_bf16[:])
+        ident_f32 = keep.tile([P, P], F32)
+        make_identity(nc, ident_f32[:])
         minus_half = keep.tile([P, 1], F32)
         nc.gpsimd.memset(minus_half[:], -0.5)
+
+        cols_ps = psum_turn.tile([P, PACK, P], BF16, tag="turn")
+        for c in range(PACK):
+            nc.tensor.transpose(cols_ps[:, c, :], vec_rows[:, c * P : (c + 1) * P], ident_bf16[:])
+        vec_cols = keep.tile([P, PACK, VECTORS], F32)
+        nc.vector.tensor_copy(out=vec_cols[:], in_=cols_ps[:, :, 0:VECTORS])
+        nc.vector.tensor_tensor(
+            out=vec_cols[:, :, 0:CODES],
+            in0=vec_cols[:, :, 0:CODES],
+            in1=vec_cols[:, :, ROW_B1 : ROW_B1 + 1].to_broadcast([P, PACK, CODES]),
+            op=ALU.add,
+        )
+        vec_all = keep.tile([P, SPREAD, CF], F32)
+        for j in range(SPREAD):
+            all_ps = psum_turn.tile([P, CF], F32, tag="turn")
+            for c in range(PACK):
+                nc.tensor.transpose(
+                    all_ps[:, c * P : (c + 1) * P],
+                    vec_cols[:, c, j : j + 1].to_broadcast([P, P]),
+                    ident_f32[:],
+                )
+            nc.scalar.copy(out=vec_all[:, j, :], in_=all_ps[:])
+        g_all = vec_all[:, ROW_G, :]
+        b_all = vec_all[:, ROW_B, :]
+        b2_all = vec_all[:, ROW_B2, :]
 
         h_words = h_sb[:].bitcast(F32)
         hT_ps = psum_once.tile([P, PASSES1, 2, P], F32)
@@ -122,16 +143,14 @@ def tile_mixtureconfounderprior_pa_s_kernel(
                 stop=(g == PASSES1 - 1),
             )
 
-        hp_b1 = keep.tile([P, CF], F32)
-        nc.vector.tensor_tensor(out=hp_b1[:], in0=hp_ps[:], in1=b1_all[:], op=ALU.add)
         mu_pre = keep.tile([P, CODES, CF], F32)
         row_sum = keep.tile([P, CODES], F32)
         for k in range(CODES):
             nc.vector.scalar_tensor_tensor(
                 out=mu_pre[:, k, :],
-                in0=hp_b1[:],
+                in0=hp_ps[:],
                 scalar=1.0,
-                in1=code_all[:, k, :],
+                in1=vec_all[:, k, :],
                 op0=ALU.mult,
                 op1=ALU.add,
                 accum_out=row_sum[:, k : k + 1],
@@ -163,7 +182,7 @@ def tile_mixtureconfounderprior_pa_s_kernel(
         for k in range(CODES):
             nc.vector.scalar_tensor_tensor(
                 out=centred_g[:, k, :], in0=mu_pre[:, k, :], scalar=neg_mean[:, k : k + 1],
-                in1=g_all[:], op0=ALU.add, op1=ALU.mult,
+                in1=g_all, op0=ALU.add, op1=ALU.mult,
             )
         mu_ln = keep.tile([P, CODES, CF], BF16)
         ln_grouped = keep.tile([P, CODES, P, PACK], BF16, align_bytes=64)
@@ -173,9 +192,9 @@ def tile_mixtureconfounderprior_pa_s_kernel(
         for k in range(CODES):
             nc.vector.scalar_tensor_tensor(
                 out=mu_ln[:, k, :], in0=centred_g[:, k, :], scalar=rstd[:, k : k + 1],
-                in1=b_all[:], op0=ALU.mult, op1=ALU.add,
+                in1=b_all, op0=ALU.mult, op1=ALU.add,
             )
-            lnT_ps = psum_turn.tile([P, PACK, P], BF16)
+            lnT_ps = psum_turn.tile([P, PACK, P], BF16, tag="turn")
             for c in range(PACK):
                 nc.tensor.transpose(
                     lnT_ps[:, c, :], mu_ln[:, k, c * P : (c + 1) * P], ident_bf16[:]
@@ -196,6 +215,6 @@ def tile_mixtureconfounderprior_pa_s_kernel(
                 start=True,
                 stop=True,
             )
-            nc.vector.tensor_tensor(out=result[:, k, :], in0=out_ps[:], in1=b2_all[:], op=ALU.add)
+            nc.vector.tensor_tensor(out=result[:, k, :], in0=out_ps[:], in1=b2_all, op=ALU.add)
             nc.scalar.activation(out=result[:, k, :], in_=result[:, k, :], func=ACT.Tanh)
             nc.sync.dma_start(out=out_rows[:, k, :], in_=result[:, k, :])

@@ -67,8 +67,10 @@ def tile_mixtureconfounderprior_pa_s_kernel(
         make_identity(nc, ident_bf16[:])
         ident_f32 = keep.tile([P, P], F32)
         make_identity(nc, ident_f32[:])
-        minus_half = keep.tile([P, 1], F32)
-        nc.gpsimd.memset(minus_half[:], -0.5)
+        eps = keep.tile([P, 1], F32)
+        nc.vector.memset(eps[:], LN_EPS)
+        table_warm = keep.tile([P, 2], F32)
+        nc.scalar.activation(out=table_warm[:, 0:1], in_=eps[:], func=ACT.Sqrt)
 
         cols_ps = psum_turn.tile([P, PACK, P], BF16, tag="turn")
         for c in range(PACK):
@@ -158,25 +160,18 @@ def tile_mixtureconfounderprior_pa_s_kernel(
         neg_mean = keep.tile([P, CODES], F32)
         squares = keep.tile([P, CODES, CF], BF16)
         sq_sum = keep.tile([P, CODES], F32)
-        var_eps = keep.tile([P, CODES], F32)
-        rstd = keep.tile([P, CODES], F32)
         for k in range(CODES):
             one = slice(k, k + 1)
-            nc.gpsimd.tensor_scalar(
-                out=neg_mean[:, one], in0=row_sum[:, one],
-                scalar1=-1.0 / CF, scalar2=0.0, op0=ALU.mult, op1=ALU.add,
-            )
+            nc.scalar.mul(out=neg_mean[:, one], in_=row_sum[:, one], mul=-1.0 / CF)
             nc.scalar.activation(
                 out=squares[:, k, :], in_=mu_pre[:, k, :], func=ACT.Square,
                 bias=neg_mean[:, one], scale=1.0, accum_out=sq_sum[:, one],
             )
-            nc.gpsimd.tensor_scalar(
-                out=var_eps[:, one], in0=sq_sum[:, one],
-                scalar1=1.0 / CF, scalar2=LN_EPS, op0=ALU.mult, op1=ALU.add,
-            )
-            nc.gpsimd.tensor_tensor(
-                out=rstd[:, one], in0=var_eps[:, one], in1=minus_half[:], op=ALU.pow
-            )
+        std = keep.tile([P, CODES], F32)
+        nc.scalar.activation(out=std[:], in_=sq_sum[:], func=ACT.Sqrt, bias=eps[:], scale=1.0 / CF)
+        nc.scalar.activation(out=table_warm[:, 1:2], in_=std[:, 0:1], func=ACT.Tanh)
+        rstd = keep.tile([P, CODES], F32)
+        nc.vector.reciprocal(out=rstd[:], in_=std[:])
 
         centred_g = keep.tile([P, CODES, CF], F32)
         for k in range(CODES):

@@ -21,7 +21,9 @@ LN_EPS = 1e-5
 
 ROW_G, ROW_B, ROW_B2, ROW_B1 = 4, 5, 6, 7
 VECTORS = 8
-SPREAD = 7
+
+QUANTISE_LAG = 2
+FINISH_LAG = 3
 
 FLOPS = 2 * P * D * CF + 2 * P * CODES * CF * CF
 
@@ -40,11 +42,18 @@ def tile_mixtureconfounderprior_pa_s_kernel(
     h_rows = h.flatten_outer_dims()
     out_rows = out.rearrange("b t k n -> (b t) k n")
 
-    with ExitStack() as pools:
-        keep = pools.enter_context(tc.tile_pool(name="keep", bufs=1))
-        psum_once = pools.enter_context(tc.psum_pool(name="psum_once", bufs=1))
-        psum_turn = pools.enter_context(tc.psum_pool(name="psum_turn", bufs=3))
-        psum_out = pools.enter_context(tc.psum_pool(name="psum_out", bufs=3))
+    with ExitStack() as stack:
+        keep = stack.enter_context(tc.tile_pool(name="keep", bufs=1))
+        psum_once = stack.enter_context(tc.psum_pool(name="psum_once", bufs=1))
+        psum_turn = stack.enter_context(tc.psum_pool(name="psum_turn", bufs=3))
+        psum_out = stack.enter_context(tc.psum_pool(name="psum_out", bufs=2))
+        stack.enter_context(tc.manual_schedule())
+
+        vec_rows = keep.tile([P, CF], BF16)
+        nc.vector.memset(vec_rows[:], 0.0)
+        nc.sync.dma_start(out=vec_rows[0:CODES, :], in_=code_mu)
+        for row, vector in ((ROW_B1, mu_b1), (ROW_G, ln_g), (ROW_B, ln_b), (ROW_B2, mu_b2)):
+            nc.sync.dma_start(out=vec_rows[row : row + 1, :], in_=vector.unsqueeze(0))
 
         h_sb = keep.tile([P, D], BF16)
         nc.sync.dma_start(out=h_sb[:], in_=h_rows)
@@ -56,12 +65,6 @@ def tile_mixtureconfounderprior_pa_s_kernel(
             )
         w2_rows = keep.tile([P, PACK, CF], BF16)
         nc.sync.dma_start(out=w2_rows[:], in_=mu_w2.rearrange("(c p) n -> p c n", p=P))
-
-        vec_rows = keep.tile([P, CF], BF16)
-        nc.vector.memset(vec_rows[:], 0.0)
-        nc.scalar.dma_start(out=vec_rows[0:CODES, :], in_=code_mu)
-        for row, vector in ((ROW_B1, mu_b1), (ROW_G, ln_g), (ROW_B, ln_b), (ROW_B2, mu_b2)):
-            nc.scalar.dma_start(out=vec_rows[row : row + 1, :], in_=vector.unsqueeze(0))
 
         ident_bf16 = keep.tile([P, P], BF16)
         make_identity(nc, ident_bf16[:])
@@ -83,55 +86,47 @@ def tile_mixtureconfounderprior_pa_s_kernel(
             in1=vec_cols[:, :, ROW_B1 : ROW_B1 + 1].to_broadcast([P, PACK, CODES]),
             op=ALU.add,
         )
-        vec_all = keep.tile([P, SPREAD, CF], F32)
-        for j in range(SPREAD):
-            all_ps = psum_turn.tile([P, CF], F32, tag="turn")
+
+        h_words = h_sb[:].bitcast(F32)
+        hT_ps = psum_turn.tile([P, PASSES1, 2, P], F32, tag="turn")
+        for g in range(PASSES1):
+            for u in range(2):
+                first = (2 * g + u) * P
+                nc.tensor.transpose(hT_ps[:, g, u, :], h_words[:, first : first + P], ident_f32[:])
+        h_grouped = keep.tile([P, PASSES1 * P * PACK], BF16, align_bytes=64)
+        nc.scalar.copy(
+            out=h_grouped[:].bitcast(F32).rearrange("p (g t u) -> p g t u", g=PASSES1, u=2),
+            in_=hT_ps[:].rearrange("p g u t -> p g t u"),
+        )
+
+        def spread(all_ps, j):
             for c in range(PACK):
                 nc.tensor.transpose(
                     all_ps[:, c * P : (c + 1) * P],
                     vec_cols[:, c, j : j + 1].to_broadcast([P, P]),
                     ident_f32[:],
                 )
-            nc.scalar.copy(out=vec_all[:, j, :], in_=all_ps[:])
-        g_all = vec_all[:, ROW_G, :]
-        b_all = vec_all[:, ROW_B, :]
-        b2_all = vec_all[:, ROW_B2, :]
 
-        h_words = h_sb[:].bitcast(F32)
-        hT_ps = psum_once.tile([P, PASSES1, 2, P], F32)
-        for g in range(PASSES1):
-            for u in range(2):
-                first = (2 * g + u) * P
-                nc.tensor.transpose(hT_ps[:, g, u, :], h_words[:, first : first + P], ident_f32[:])
-        h_grouped = keep.tile([P, PASSES1 * P * PACK], BF16, align_bytes=64)
-        nc.vector.tensor_copy(
-            out=h_grouped[:].bitcast(F32).rearrange("p (g t u) -> p g t u", g=PASSES1, u=2),
-            in_=hT_ps[:].rearrange("p g u t -> p g t u"),
-        )
+        c_all = keep.tile([P, CODES, CF], F32)
+        for k in range(CODES):
+            c_ps = psum_turn.tile([P, CF], F32, tag="turn")
+            spread(c_ps, k)
+            nc.scalar.copy(out=c_all[:, k, :], in_=c_ps[:])
+
         h_codes = keep.tile([P, PASSES1 * P], U32, align_bytes=64)
         h_scales = keep.tile([P, PASSES1 * P], U8, align_bytes=64)
-        nc.vector.quantize_mx(out=h_codes[:].bitcast(FP8X4), scales=h_scales[:], in_=h_grouped[:])
-
         w1_grouped = keep.tile([P, PASSES1, CF, PACK], BF16, align_bytes=64)
         w1_codes = keep.tile([P, PASSES1, CF], U32, align_bytes=64)
         w1_scales = keep.tile([P, PASSES1, CF], U8, align_bytes=64)
-        for g in range(PASSES1):
-            regroup(nc.vector.tensor_copy, w1_grouped[:, g], w1_rows[:, g])
+        regroup(nc.vector.tensor_copy, w1_grouped[:, 0], w1_rows[:, 0])
+        nc.vector.quantize_mx(out=h_codes[:].bitcast(FP8X4), scales=h_scales[:], in_=h_grouped[:])
+        regroup(nc.vector.tensor_copy, w1_grouped[:, 1], w1_rows[:, 1])
         for g in range(PASSES1):
             nc.vector.quantize_mx(
                 out=w1_codes[:, g, :].bitcast(FP8X4),
                 scales=w1_scales[:, g, :],
                 in_=w1_grouped[:, g].rearrange("p n j -> p (n j)"),
             )
-        w2_grouped = keep.tile([P, CF, PACK], BF16, align_bytes=64)
-        w2_codes = keep.tile([P, CF], U32, align_bytes=64)
-        w2_scales = keep.tile([P, CF], U8, align_bytes=64)
-        regroup(nc.scalar.copy, w2_grouped[:], w2_rows[:])
-        nc.vector.quantize_mx(
-            out=w2_codes[:].bitcast(FP8X4),
-            scales=w2_scales[:],
-            in_=w2_grouped[:].rearrange("p n j -> p (n j)"),
-        )
 
         hp_ps = psum_once.tile([P, CF], F32)
         for g in range(PASSES1):
@@ -144,50 +139,65 @@ def tile_mixtureconfounderprior_pa_s_kernel(
                 start=(g == 0),
                 stop=(g == PASSES1 - 1),
             )
+        g_all = psum_once.tile([P, CF], F32)
+        spread(g_all, ROW_G)
+        b_all = psum_once.tile([P, CF], F32)
+        spread(b_all, ROW_B)
+        b2_ps = psum_turn.tile([P, CF], F32, tag="turn")
+        spread(b2_ps, ROW_B2)
+
+        w2_grouped = keep.tile([P, CF, PACK], BF16, align_bytes=64)
+        w2_codes = keep.tile([P, CF], U32, align_bytes=64)
+        w2_scales = keep.tile([P, CF], U8, align_bytes=64)
+        regroup(nc.scalar.copy, w2_grouped[:], w2_rows[:])
 
         mu_pre = keep.tile([P, CODES, CF], F32)
         row_sum = keep.tile([P, CODES], F32)
-        for k in range(CODES):
-            nc.vector.scalar_tensor_tensor(
-                out=mu_pre[:, k, :],
-                in0=hp_ps[:],
-                scalar=1.0,
-                in1=vec_all[:, k, :],
-                op0=ALU.mult,
-                op1=ALU.add,
-                accum_out=row_sum[:, k : k + 1],
-            )
         neg_mean = keep.tile([P, CODES], F32)
         squares = keep.tile([P, CODES, CF], BF16)
         sq_sum = keep.tile([P, CODES], F32)
         for k in range(CODES):
             one = slice(k, k + 1)
+            nc.vector.scalar_tensor_tensor(
+                out=mu_pre[:, k, :], in0=hp_ps[:], scalar=1.0, in1=c_all[:, k, :],
+                op0=ALU.mult, op1=ALU.add, accum_out=row_sum[:, one],
+            )
             nc.scalar.mul(out=neg_mean[:, one], in_=row_sum[:, one], mul=-1.0 / CF)
             nc.scalar.activation(
                 out=squares[:, k, :], in_=mu_pre[:, k, :], func=ACT.Square,
                 bias=neg_mean[:, one], scale=1.0, accum_out=sq_sum[:, one],
             )
+        nc.vector.quantize_mx(
+            out=w2_codes[:].bitcast(FP8X4),
+            scales=w2_scales[:],
+            in_=w2_grouped[:].rearrange("p n j -> p (n j)"),
+        )
         std = keep.tile([P, CODES], F32)
         nc.scalar.activation(out=std[:], in_=sq_sum[:], func=ACT.Sqrt, bias=eps[:], scale=1.0 / CF)
         nc.scalar.activation(out=table_warm[:, 1:2], in_=std[:, 0:1], func=ACT.Tanh)
-        rstd = keep.tile([P, CODES], F32)
-        nc.vector.reciprocal(out=rstd[:], in_=std[:])
+        b2_all = keep.tile([P, CF], F32)
+        nc.scalar.copy(out=b2_all[:], in_=b2_ps[:])
 
         centred_g = keep.tile([P, CODES, CF], F32)
         for k in range(CODES):
             nc.vector.scalar_tensor_tensor(
                 out=centred_g[:, k, :], in0=mu_pre[:, k, :], scalar=neg_mean[:, k : k + 1],
-                in1=g_all, op0=ALU.add, op1=ALU.mult,
+                in1=g_all[:], op0=ALU.add, op1=ALU.mult,
             )
+        rstd = keep.tile([P, CODES], F32)
+        nc.vector.reciprocal(out=rstd[:], in_=std[:])
+
         mu_ln = keep.tile([P, CODES, CF], BF16)
         ln_grouped = keep.tile([P, CODES, P, PACK], BF16, align_bytes=64)
         ln_codes = keep.tile([P, CODES, P], U32, align_bytes=64)
         ln_scales = keep.tile([P, CODES, P], U8, align_bytes=64)
+        out_banks = {}
         result = keep.tile([P, CODES, CF], F32)
-        for k in range(CODES):
+
+        def normalise_and_turn(k):
             nc.vector.scalar_tensor_tensor(
                 out=mu_ln[:, k, :], in0=centred_g[:, k, :], scalar=rstd[:, k : k + 1],
-                in1=b_all, op0=ALU.mult, op1=ALU.add,
+                in1=b_all[:], op0=ALU.mult, op1=ALU.add,
             )
             lnT_ps = psum_turn.tile([P, PACK, P], BF16, tag="turn")
             for c in range(PACK):
@@ -195,12 +205,15 @@ def tile_mixtureconfounderprior_pa_s_kernel(
                     lnT_ps[:, c, :], mu_ln[:, k, c * P : (c + 1) * P], ident_bf16[:]
                 )
             nc.scalar.copy(out=ln_grouped[:, k], in_=lnT_ps[:].rearrange("p c t -> p t c"))
+
+        def quantise_and_multiply(k):
             nc.vector.quantize_mx(
                 out=ln_codes[:, k, :].bitcast(FP8X4),
                 scales=ln_scales[:, k, :],
                 in_=ln_grouped[:, k].rearrange("p t c -> p (t c)"),
             )
             out_ps = psum_out.tile([P, CF], F32)
+            out_banks[k] = out_ps
             nc.tensor.matmul_mx(
                 out=out_ps[:],
                 lhsT=ln_codes[:, k, :].bitcast(FP8X4),
@@ -210,6 +223,18 @@ def tile_mixtureconfounderprior_pa_s_kernel(
                 start=True,
                 stop=True,
             )
-            nc.vector.tensor_tensor(out=result[:, k, :], in0=out_ps[:], in1=b2_all, op=ALU.add)
+
+        def finish(k):
+            nc.vector.tensor_tensor(
+                out=result[:, k, :], in0=out_banks[k][:], in1=b2_all[:], op=ALU.add
+            )
             nc.scalar.activation(out=result[:, k, :], in_=result[:, k, :], func=ACT.Tanh)
             nc.sync.dma_start(out=out_rows[:, k, :], in_=result[:, k, :])
+
+        for step in range(CODES + FINISH_LAG):
+            if step < CODES:
+                normalise_and_turn(step)
+            if 0 <= step - QUANTISE_LAG < CODES:
+                quantise_and_multiply(step - QUANTISE_LAG)
+            if step >= FINISH_LAG:
+                finish(step - FINISH_LAG)

@@ -22,6 +22,8 @@ LN_EPS = 1e-5
 ROW_G, ROW_B, ROW_B2, ROW_B1 = 4, 5, 6, 7
 VECTORS = 8
 
+SPREAD_AHEAD = 2
+W1_VECTOR_COLS = 352
 QUANTISE_LAG = 2
 FINISH_LAG = 3
 
@@ -50,7 +52,7 @@ def tile_mixtureconfounderprior_pa_s_kernel(
         stack.enter_context(tc.manual_schedule())
 
         vec_rows = keep.tile([P, CF], BF16)
-        nc.vector.memset(vec_rows[:], 0.0)
+        nc.gpsimd.memset(vec_rows[:].bitcast(F32), 0.0)
         nc.sync.dma_start(out=vec_rows[0:CODES, :], in_=code_mu)
         for row, vector in ((ROW_B1, mu_b1), (ROW_G, ln_g), (ROW_B, ln_b), (ROW_B2, mu_b2)):
             nc.sync.dma_start(out=vec_rows[row : row + 1, :], in_=vector.unsqueeze(0))
@@ -65,6 +67,11 @@ def tile_mixtureconfounderprior_pa_s_kernel(
             )
         w2_rows = keep.tile([P, PACK, CF], BF16)
         nc.sync.dma_start(out=w2_rows[:], in_=mu_w2.rearrange("(c p) n -> p c n", p=P))
+
+        def gpsimd_copy(out, in_):
+            nc.gpsimd.tensor_scalar(
+                out=out, in0=in_, scalar1=1.0, scalar2=0.0, op0=ALU.mult, op1=ALU.add
+            )
 
         ident_bf16 = keep.tile([P, P], BF16)
         make_identity(nc, ident_bf16[:])
@@ -108,25 +115,50 @@ def tile_mixtureconfounderprior_pa_s_kernel(
                 )
 
         c_all = keep.tile([P, CODES, CF], F32)
-        for k in range(CODES):
+
+        def spread_code(k):
             c_ps = psum_turn.tile([P, CF], F32, tag="turn")
             spread(c_ps, k)
             nc.scalar.copy(out=c_all[:, k, :], in_=c_ps[:])
+
+
+        w2_grouped = keep.tile([P, CF, PACK], BF16, align_bytes=64)
+        w2_codes = keep.tile([P, CF], U32, align_bytes=64)
+        w2_scales = keep.tile([P, CF], U8, align_bytes=64)
+        regroup(gpsimd_copy, w2_grouped[:], w2_rows[:])
 
         h_codes = keep.tile([P, PASSES1 * P], U32, align_bytes=64)
         h_scales = keep.tile([P, PASSES1 * P], U8, align_bytes=64)
         w1_grouped = keep.tile([P, PASSES1, CF, PACK], BF16, align_bytes=64)
         w1_codes = keep.tile([P, PASSES1, CF], U32, align_bytes=64)
         w1_scales = keep.tile([P, PASSES1, CF], U8, align_bytes=64)
-        regroup(nc.vector.tensor_copy, w1_grouped[:, 0], w1_rows[:, 0])
-        nc.vector.quantize_mx(out=h_codes[:].bitcast(FP8X4), scales=h_scales[:], in_=h_grouped[:])
-        regroup(nc.vector.tensor_copy, w1_grouped[:, 1], w1_rows[:, 1])
-        for g in range(PASSES1):
+
+        def quantise_w1(g):
             nc.vector.quantize_mx(
                 out=w1_codes[:, g, :].bitcast(FP8X4),
                 scales=w1_scales[:, g, :],
                 in_=w1_grouped[:, g].rearrange("p n j -> p (n j)"),
             )
+
+        def regroup_w1(g):
+            regroup(
+                nc.vector.tensor_copy,
+                w1_grouped[:, g, 0:W1_VECTOR_COLS],
+                w1_rows[:, g, :, 0:W1_VECTOR_COLS],
+            )
+            regroup(
+                nc.scalar.copy,
+                w1_grouped[:, g, W1_VECTOR_COLS:CF],
+                w1_rows[:, g, :, W1_VECTOR_COLS:CF],
+            )
+
+        regroup_w1(0)
+        spread_code(0)
+        nc.vector.quantize_mx(out=h_codes[:].bitcast(FP8X4), scales=h_scales[:], in_=h_grouped[:])
+        quantise_w1(0)
+        regroup_w1(1)
+        spread_code(1)
+        quantise_w1(1)
 
         hp_ps = psum_once.tile([P, CF], F32)
         for g in range(PASSES1):
@@ -139,17 +171,14 @@ def tile_mixtureconfounderprior_pa_s_kernel(
                 start=(g == 0),
                 stop=(g == PASSES1 - 1),
             )
+        for k in range(SPREAD_AHEAD, CODES):
+            spread_code(k)
         g_all = psum_once.tile([P, CF], F32)
         spread(g_all, ROW_G)
         b_all = psum_once.tile([P, CF], F32)
         spread(b_all, ROW_B)
         b2_ps = psum_turn.tile([P, CF], F32, tag="turn")
         spread(b2_ps, ROW_B2)
-
-        w2_grouped = keep.tile([P, CF, PACK], BF16, align_bytes=64)
-        w2_codes = keep.tile([P, CF], U32, align_bytes=64)
-        w2_scales = keep.tile([P, CF], U8, align_bytes=64)
-        regroup(nc.scalar.copy, w2_grouped[:], w2_rows[:])
 
         mu_pre = keep.tile([P, CODES, CF], F32)
         row_sum = keep.tile([P, CODES], F32)
@@ -167,11 +196,6 @@ def tile_mixtureconfounderprior_pa_s_kernel(
                 out=squares[:, k, :], in_=mu_pre[:, k, :], func=ACT.Square,
                 bias=neg_mean[:, one], scale=1.0, accum_out=sq_sum[:, one],
             )
-        nc.vector.quantize_mx(
-            out=w2_codes[:].bitcast(FP8X4),
-            scales=w2_scales[:],
-            in_=w2_grouped[:].rearrange("p n j -> p (n j)"),
-        )
         std = keep.tile([P, CODES], F32)
         nc.scalar.activation(out=std[:], in_=sq_sum[:], func=ACT.Sqrt, bias=eps[:], scale=1.0 / CF)
         nc.scalar.activation(out=table_warm[:, 1:2], in_=std[:, 0:1], func=ACT.Tanh)
@@ -186,6 +210,11 @@ def tile_mixtureconfounderprior_pa_s_kernel(
             )
         rstd = keep.tile([P, CODES], F32)
         nc.vector.reciprocal(out=rstd[:], in_=std[:])
+        nc.vector.quantize_mx(
+            out=w2_codes[:].bitcast(FP8X4),
+            scales=w2_scales[:],
+            in_=w2_grouped[:].rearrange("p n j -> p (n j)"),
+        )
 
         mu_ln = keep.tile([P, CODES, CF], BF16)
         ln_grouped = keep.tile([P, CODES, P, PACK], BF16, align_bytes=64)

@@ -23,7 +23,6 @@ ROW_G, ROW_B, ROW_B2, ROW_B1 = 4, 5, 6, 7
 VECTORS = 8
 
 SPREAD_AHEAD = 2
-W1_VECTOR_COLS = 352
 QUANTISE_LAG = 2
 FINISH_LAG = 3
 
@@ -52,7 +51,7 @@ def tile_mixtureconfounderprior_pa_s_kernel(
         stack.enter_context(tc.manual_schedule())
 
         vec_rows = keep.tile([P, CF], BF16)
-        nc.gpsimd.memset(vec_rows[:].bitcast(F32), 0.0)
+        nc.vector.memset(vec_rows[:], 0.0)
         nc.sync.dma_start(out=vec_rows[0:CODES, :], in_=code_mu)
         for row, vector in ((ROW_B1, mu_b1), (ROW_G, ln_g), (ROW_B, ln_b), (ROW_B2, mu_b2)):
             nc.sync.dma_start(out=vec_rows[row : row + 1, :], in_=vector.unsqueeze(0))
@@ -67,11 +66,6 @@ def tile_mixtureconfounderprior_pa_s_kernel(
             )
         w2_rows = keep.tile([P, PACK, CF], BF16)
         nc.sync.dma_start(out=w2_rows[:], in_=mu_w2.rearrange("(c p) n -> p c n", p=P))
-
-        def gpsimd_copy(out, in_):
-            nc.gpsimd.tensor_scalar(
-                out=out, in0=in_, scalar1=1.0, scalar2=0.0, op0=ALU.mult, op1=ALU.add
-            )
 
         ident_bf16 = keep.tile([P, P], BF16)
         make_identity(nc, ident_bf16[:])
@@ -94,6 +88,19 @@ def tile_mixtureconfounderprior_pa_s_kernel(
             op=ALU.add,
         )
 
+        def spread(all_ps, j):
+            for c in range(PACK):
+                nc.tensor.transpose(
+                    all_ps[:, c * P : (c + 1) * P],
+                    vec_cols[:, c, j : j + 1].to_broadcast([P, P]),
+                    ident_f32[:],
+                )
+
+        b2_ps = psum_turn.tile([P, CF], F32, tag="turn")
+        spread(b2_ps, ROW_B2)
+        b2_all = keep.tile([P, CF], F32)
+        nc.scalar.copy(out=b2_all[:], in_=b2_ps[:])
+
         h_words = h_sb[:].bitcast(F32)
         hT_ps = psum_turn.tile([P, PASSES1, 2, P], F32, tag="turn")
         for g in range(PASSES1):
@@ -106,14 +113,6 @@ def tile_mixtureconfounderprior_pa_s_kernel(
             in_=hT_ps[:].rearrange("p g u t -> p g t u"),
         )
 
-        def spread(all_ps, j):
-            for c in range(PACK):
-                nc.tensor.transpose(
-                    all_ps[:, c * P : (c + 1) * P],
-                    vec_cols[:, c, j : j + 1].to_broadcast([P, P]),
-                    ident_f32[:],
-                )
-
         c_all = keep.tile([P, CODES, CF], F32)
 
         def spread_code(k):
@@ -121,44 +120,28 @@ def tile_mixtureconfounderprior_pa_s_kernel(
             spread(c_ps, k)
             nc.scalar.copy(out=c_all[:, k, :], in_=c_ps[:])
 
+        for k in range(SPREAD_AHEAD):
+            spread_code(k)
 
         w2_grouped = keep.tile([P, CF, PACK], BF16, align_bytes=64)
         w2_codes = keep.tile([P, CF], U32, align_bytes=64)
         w2_scales = keep.tile([P, CF], U8, align_bytes=64)
-        regroup(gpsimd_copy, w2_grouped[:], w2_rows[:])
+        regroup(nc.scalar.copy, w2_grouped[:], w2_rows[:])
 
         h_codes = keep.tile([P, PASSES1 * P], U32, align_bytes=64)
         h_scales = keep.tile([P, PASSES1 * P], U8, align_bytes=64)
         w1_grouped = keep.tile([P, PASSES1, CF, PACK], BF16, align_bytes=64)
         w1_codes = keep.tile([P, PASSES1, CF], U32, align_bytes=64)
         w1_scales = keep.tile([P, PASSES1, CF], U8, align_bytes=64)
-
-        def quantise_w1(g):
+        regroup(nc.vector.tensor_copy, w1_grouped[:, 0], w1_rows[:, 0])
+        nc.vector.quantize_mx(out=h_codes[:].bitcast(FP8X4), scales=h_scales[:], in_=h_grouped[:])
+        regroup(nc.vector.tensor_copy, w1_grouped[:, 1], w1_rows[:, 1])
+        for g in range(PASSES1):
             nc.vector.quantize_mx(
                 out=w1_codes[:, g, :].bitcast(FP8X4),
                 scales=w1_scales[:, g, :],
                 in_=w1_grouped[:, g].rearrange("p n j -> p (n j)"),
             )
-
-        def regroup_w1(g):
-            regroup(
-                nc.vector.tensor_copy,
-                w1_grouped[:, g, 0:W1_VECTOR_COLS],
-                w1_rows[:, g, :, 0:W1_VECTOR_COLS],
-            )
-            regroup(
-                nc.scalar.copy,
-                w1_grouped[:, g, W1_VECTOR_COLS:CF],
-                w1_rows[:, g, :, W1_VECTOR_COLS:CF],
-            )
-
-        regroup_w1(0)
-        spread_code(0)
-        nc.vector.quantize_mx(out=h_codes[:].bitcast(FP8X4), scales=h_scales[:], in_=h_grouped[:])
-        quantise_w1(0)
-        regroup_w1(1)
-        spread_code(1)
-        quantise_w1(1)
 
         hp_ps = psum_once.tile([P, CF], F32)
         for g in range(PASSES1):
@@ -177,14 +160,19 @@ def tile_mixtureconfounderprior_pa_s_kernel(
         spread(g_all, ROW_G)
         b_all = psum_once.tile([P, CF], F32)
         spread(b_all, ROW_B)
-        b2_ps = psum_turn.tile([P, CF], F32, tag="turn")
-        spread(b2_ps, ROW_B2)
 
         mu_pre = keep.tile([P, CODES, CF], F32)
         row_sum = keep.tile([P, CODES], F32)
         neg_mean = keep.tile([P, CODES], F32)
         squares = keep.tile([P, CODES, CF], BF16)
         sq_sum = keep.tile([P, CODES], F32)
+
+        def sum_of_squares(k):
+            nc.scalar.activation(
+                out=squares[:, k, :], in_=mu_pre[:, k, :], func=ACT.Square,
+                bias=neg_mean[:, k : k + 1], scale=1.0, accum_out=sq_sum[:, k : k + 1],
+            )
+
         for k in range(CODES):
             one = slice(k, k + 1)
             nc.vector.scalar_tensor_tensor(
@@ -192,15 +180,12 @@ def tile_mixtureconfounderprior_pa_s_kernel(
                 op0=ALU.mult, op1=ALU.add, accum_out=row_sum[:, one],
             )
             nc.scalar.mul(out=neg_mean[:, one], in_=row_sum[:, one], mul=-1.0 / CF)
-            nc.scalar.activation(
-                out=squares[:, k, :], in_=mu_pre[:, k, :], func=ACT.Square,
-                bias=neg_mean[:, one], scale=1.0, accum_out=sq_sum[:, one],
-            )
+            if k > 0:
+                sum_of_squares(k - 1)
+        sum_of_squares(CODES - 1)
         std = keep.tile([P, CODES], F32)
         nc.scalar.activation(out=std[:], in_=sq_sum[:], func=ACT.Sqrt, bias=eps[:], scale=1.0 / CF)
         nc.scalar.activation(out=table_warm[:, 1:2], in_=std[:, 0:1], func=ACT.Tanh)
-        b2_all = keep.tile([P, CF], F32)
-        nc.scalar.copy(out=b2_all[:], in_=b2_ps[:])
 
         centred_g = keep.tile([P, CODES, CF], F32)
         for k in range(CODES):

from contextlib import ExitStack

import concourse.mybir as mybir
from concourse.masks import make_identity

F32 = mybir.dt.float32
BF16 = mybir.dt.bfloat16
U32 = mybir.dt.uint32
U8 = mybir.dt.uint8
FP8X4 = mybir.dt.float8_e4m3fn_x4
ALU = mybir.AluOpType
ACT = mybir.ActivationFunctionType

P = 128
PACK = 4
D = 1024
PASSES1 = D // (P * PACK)
CODES = 4
CF = 512
LN_EPS = 1e-5

ROW_G, ROW_B, ROW_B2, ROW_B1 = 4, 5, 6, 7
VECTORS = 8

SPREAD_AHEAD = 2
QUANTISE_LAG = 2
FINISH_LAG = 3

FLOPS = 2 * P * D * CF + 2 * P * CODES * CF * CF


def regroup(copy, grouped, rows):
    copy(
        out=grouped.rearrange("p (c i) j -> p c j i", i=4),
        in_=rows.rearrange("p j (c i) -> p c j i", i=4),
    )


def tile_mixtureconfounderprior_pa_s_kernel(
    tc, h, mu_w1_h, code_mu, mu_b1, ln_g, ln_b, mu_w2, mu_b2, out
):
    nc = tc.nc
    h_rows = h.flatten_outer_dims()
    out_rows = out.rearrange("b t k n -> (b t) k n")

    with ExitStack() as stack:
        keep = stack.enter_context(tc.tile_pool(name="keep", bufs=1))
        psum_once = stack.enter_context(tc.psum_pool(name="psum_once", bufs=1))
        psum_turn = stack.enter_context(tc.psum_pool(name="psum_turn", bufs=3))
        psum_out = stack.enter_context(tc.psum_pool(name="psum_out", bufs=2))
        stack.enter_context(tc.manual_schedule())

        vec_rows = keep.tile([P, CF], BF16)
        nc.vector.memset(vec_rows[:], 0.0)
        nc.sync.dma_start(out=vec_rows[0:CODES, :], in_=code_mu)
        for row, vector in ((ROW_B1, mu_b1), (ROW_G, ln_g), (ROW_B, ln_b), (ROW_B2, mu_b2)):
            nc.sync.dma_start(out=vec_rows[row : row + 1, :], in_=vector.unsqueeze(0))

        h_sb = keep.tile([P, D], BF16)
        nc.sync.dma_start(out=h_sb[:], in_=h_rows)
        w1_rows = keep.tile([P, PASSES1, PACK, CF], BF16)
        w1_view = mu_w1_h.rearrange("(g u q e) n -> g q u (e n)", g=PASSES1, u=2, e=2)
        for g in range(PASSES1):
            nc.sync.dma_start(
                out=w1_rows[:, g].rearrange("p (u e) n -> p u (e n)", u=2), in_=w1_view[g]
            )
        w2_rows = keep.tile([P, PACK, CF], BF16)
        nc.sync.dma_start(out=w2_rows[:], in_=mu_w2.rearrange("(c p) n -> p c n", p=P))

        ident_bf16 = keep.tile([P, P], BF16)
        make_identity(nc, ident_bf16[:])
        ident_f32 = keep.tile([P, P], F32)
        make_identity(nc, ident_f32[:])
        eps = keep.tile([P, 1], F32)
        nc.vector.memset(eps[:], LN_EPS)
        table_warm = keep.tile([P, 2], F32)
        nc.scalar.activation(out=table_warm[:, 0:1], in_=eps[:], func=ACT.Sqrt)

        cols_ps = psum_turn.tile([P, PACK, P], BF16, tag="turn")
        for c in range(PACK):
            nc.tensor.transpose(cols_ps[:, c, :], vec_rows[:, c * P : (c + 1) * P], ident_bf16[:])
        vec_cols = keep.tile([P, PACK, VECTORS], F32)
        nc.vector.tensor_copy(out=vec_cols[:], in_=cols_ps[:, :, 0:VECTORS])
        nc.vector.tensor_tensor(
            out=vec_cols[:, :, 0:CODES],
            in0=vec_cols[:, :, 0:CODES],
            in1=vec_cols[:, :, ROW_B1 : ROW_B1 + 1].to_broadcast([P, PACK, CODES]),
            op=ALU.add,
        )

        def spread(all_ps, j):
            for c in range(PACK):
                nc.tensor.transpose(
                    all_ps[:, c * P : (c + 1) * P],
                    vec_cols[:, c, j : j + 1].to_broadcast([P, P]),
                    ident_f32[:],
                )

        b2_ps = psum_turn.tile([P, CF], F32, tag="turn")
        spread(b2_ps, ROW_B2)
        b2_all = keep.tile([P, CF], F32)
        nc.scalar.copy(out=b2_all[:], in_=b2_ps[:])

        h_words = h_sb[:].bitcast(F32)
        hT_ps = psum_turn.tile([P, PASSES1, 2, P], F32, tag="turn")
        for g in range(PASSES1):
            for u in range(2):
                first = (2 * g + u) * P
                nc.tensor.transpose(hT_ps[:, g, u, :], h_words[:, first : first + P], ident_f32[:])
        h_grouped = keep.tile([P, PASSES1 * P * PACK], BF16, align_bytes=64)
        nc.scalar.copy(
            out=h_grouped[:].bitcast(F32).rearrange("p (g t u) -> p g t u", g=PASSES1, u=2),
            in_=hT_ps[:].rearrange("p g u t -> p g t u"),
        )

        c_all = keep.tile([P, CODES, CF], F32)

        def spread_code(k):
            c_ps = psum_turn.tile([P, CF], F32, tag="turn")
            spread(c_ps, k)
            nc.scalar.copy(out=c_all[:, k, :], in_=c_ps[:])

        for k in range(SPREAD_AHEAD):
            spread_code(k)

        w2_grouped = keep.tile([P, CF, PACK], BF16, align_bytes=64)
        w2_codes = keep.tile([P, CF], U32, align_bytes=64)
        w2_scales = keep.tile([P, CF], U8, align_bytes=64)
        regroup(nc.scalar.copy, w2_grouped[:], w2_rows[:])

        h_codes = keep.tile([P, PASSES1 * P], U32, align_bytes=64)
        h_scales = keep.tile([P, PASSES1 * P], U8, align_bytes=64)
        w1_grouped = keep.tile([P, PASSES1, CF, PACK], BF16, align_bytes=64)
        w1_codes = keep.tile([P, PASSES1, CF], U32, align_bytes=64)
        w1_scales = keep.tile([P, PASSES1, CF], U8, align_bytes=64)
        regroup(nc.vector.tensor_copy, w1_grouped[:, 0], w1_rows[:, 0])
        nc.vector.quantize_mx(out=h_codes[:].bitcast(FP8X4), scales=h_scales[:], in_=h_grouped[:])
        regroup(nc.vector.tensor_copy, w1_grouped[:, 1], w1_rows[:, 1])
        for g in range(PASSES1):
            nc.vector.quantize_mx(
                out=w1_codes[:, g, :].bitcast(FP8X4),
                scales=w1_scales[:, g, :],
                in_=w1_grouped[:, g].rearrange("p n j -> p (n j)"),
            )

        hp_ps = psum_once.tile([P, CF], F32)
        for g in range(PASSES1):
            nc.tensor.matmul_mx(
                out=hp_ps[:],
                lhsT=h_codes[:, g * P : (g + 1) * P].bitcast(FP8X4),
                lhsT_scale=h_scales[:, g * P : (g + 1) * P],
                rhs=w1_codes[:, g, :].bitcast(FP8X4),
                rhs_scale=w1_scales[:, g, :],
                start=(g == 0),
                stop=(g == PASSES1 - 1),
            )
        for k in range(SPREAD_AHEAD, CODES):
            spread_code(k)
        g_all = psum_once.tile([P, CF], F32)
        spread(g_all, ROW_G)
        b_all = psum_once.tile([P, CF], F32)
        spread(b_all, ROW_B)

        mu_pre = keep.tile([P, CODES, CF], F32)
        row_sum = keep.tile([P, CODES], F32)
        neg_mean = keep.tile([P, CODES], F32)
        squares = keep.tile([P, CODES, CF], BF16)
        sq_sum = keep.tile([P, CODES], F32)

        def sum_of_squares(k):
            nc.scalar.activation(
                out=squares[:, k, :], in_=mu_pre[:, k, :], func=ACT.Square,
                bias=neg_mean[:, k : k + 1], scale=1.0, accum_out=sq_sum[:, k : k + 1],
            )

        for k in range(CODES):
            one = slice(k, k + 1)
            nc.vector.scalar_tensor_tensor(
                out=mu_pre[:, k, :], in0=hp_ps[:], scalar=1.0, in1=c_all[:, k, :],
                op0=ALU.mult, op1=ALU.add, accum_out=row_sum[:, one],
            )
            nc.scalar.mul(out=neg_mean[:, one], in_=row_sum[:, one], mul=-1.0 / CF)
            if k > 0:
                sum_of_squares(k - 1)
        sum_of_squares(CODES - 1)
        std = keep.tile([P, CODES], F32)
        nc.scalar.activation(out=std[:], in_=sq_sum[:], func=ACT.Sqrt, bias=eps[:], scale=1.0 / CF)
        nc.scalar.activation(out=table_warm[:, 1:2], in_=std[:, 0:1], func=ACT.Tanh)

        centred_g = keep.tile([P, CODES, CF], F32)
        for k in range(CODES):
            nc.vector.scalar_tensor_tensor(
                out=centred_g[:, k, :], in0=mu_pre[:, k, :], scalar=neg_mean[:, k : k + 1],
                in1=g_all[:], op0=ALU.add, op1=ALU.mult,
            )
        rstd = keep.tile([P, CODES], F32)
        nc.vector.reciprocal(out=rstd[:], in_=std[:])
        nc.vector.quantize_mx(
            out=w2_codes[:].bitcast(FP8X4),
            scales=w2_scales[:],
            in_=w2_grouped[:].rearrange("p n j -> p (n j)"),
        )

        mu_ln = keep.tile([P, CODES, CF], BF16)
        ln_grouped = keep.tile([P, CODES, P, PACK], BF16, align_bytes=64)
        ln_codes = keep.tile([P, CODES, P], U32, align_bytes=64)
        ln_scales = keep.tile([P, CODES, P], U8, align_bytes=64)
        out_banks = {}
        result = keep.tile([P, CODES, CF], F32)

        def normalise_and_turn(k):
            nc.vector.scalar_tensor_tensor(
                out=mu_ln[:, k, :], in0=centred_g[:, k, :], scalar=rstd[:, k : k + 1],
                in1=b_all[:], op0=ALU.mult, op1=ALU.add,
            )
            lnT_ps = psum_turn.tile([P, PACK, P], BF16, tag="turn")
            for c in range(PACK):
                nc.tensor.transpose(
                    lnT_ps[:, c, :], mu_ln[:, k, c * P : (c + 1) * P], ident_bf16[:]
                )
            nc.scalar.copy(out=ln_grouped[:, k], in_=lnT_ps[:].rearrange("p c t -> p t c"))

        def quantise_and_multiply(k):
            nc.vector.quantize_mx(
                out=ln_codes[:, k, :].bitcast(FP8X4),
                scales=ln_scales[:, k, :],
                in_=ln_grouped[:, k].rearrange("p t c -> p (t c)"),
            )
            out_ps = psum_out.tile([P, CF], F32)
            out_banks[k] = out_ps
            nc.tensor.matmul_mx(
                out=out_ps[:],
                lhsT=ln_codes[:, k, :].bitcast(FP8X4),
                lhsT_scale=ln_scales[:, k, :],
                rhs=w2_codes[:].bitcast(FP8X4),
                rhs_scale=w2_scales[:],
                start=True,
                stop=True,
            )

        def finish(k):
            nc.vector.tensor_tensor(
                out=result[:, k, :], in0=out_banks[k][:], in1=b2_all[:], op=ALU.add
            )
            nc.scalar.activation(out=result[:, k, :], in_=result[:, k, :], func=ACT.Tanh)
            nc.sync.dma_start(out=out_rows[:, k, :], in_=result[:, k, :])

        for step in range(CODES + FINISH_LAG):
            if step < CODES:
                normalise_and_turn(step)
            if 0 <= step - QUANTISE_LAG < CODES:
                quantise_and_multiply(step - QUANTISE_LAG)
            if step >= FINISH_LAG:
                finish(step - FINISH_LAG)
